import numpy as np
import ml_dtypes


def mxq(x, axis, fmt="e4m3"):
    dtype, down = {"e4m3": (ml_dtypes.float8_e4m3fn, 7), "e5m2": (ml_dtypes.float8_e5m2, 14)}[fmt]
    v = np.moveaxis(np.asarray(x, np.float32).astype(ml_dtypes.bfloat16).astype(np.float64), axis, -1)
    blocks = v.reshape(v.shape[:-1] + (-1, 32))
    amax = np.abs(blocks).max(-1, keepdims=True)
    byte = np.maximum(np.where(amax > 0, np.frexp(amax)[1] - 1 + 127, 0) - down, 1)
    scale = np.exp2(byte - 127.0)
    codes = (blocks / scale).astype(np.float32).astype(dtype).astype(np.float64)
    return np.moveaxis((codes * scale).reshape(v.shape), -1, axis)


WIDE = False


def mx_kscale(k):
    if not WIDE:
        return np.ones(k)
    levels = np.array([10, -10, 5, -5, 0])
    a = np.random.permutation(np.resize(levels, k // 512 * 4)).reshape(k // 512, 4)
    idx = np.arange(k)
    return np.exp2(a[idx // 512, idx % 128 // 32])


BF16 = ml_dtypes.bfloat16


def bf(x):
    return np.asarray(x, np.float32).astype(BF16)


def f64(x):
    return np.asarray(x).astype(np.float64)


B, L, D, O = 16, 256, 512, 2


def setup_inputs():
    s = mx_kscale(D)
    u = mx_kscale(D)
    w = np.random.standard_normal((O, D + 1, D))
    w[:, :D, :] *= 3.0 / D / s[:, None]
    w[:, D, :] *= 1.0 / np.sqrt(D)
    return {"x1": bf(np.random.standard_normal((B, L, D)) * s),
            "x2": bf(np.random.standard_normal((B, L, D)) / u),
            "bw": bf(np.random.uniform(size=(2,))),
            "W_bil": bf(w * u),
            "t_ones": bf(np.random.standard_normal((B, L, O))),
            "lin1": bf(np.random.standard_normal((B, L, O))),
            "lin2": bf(np.random.standard_normal((B, L, O))),
            "b_lin": bf(np.random.standard_normal(O) * 0.5)}


def reference(x1, x2, bw, W_bil, t_ones, lin1, lin2, b_lin):
    e = np.exp(f64(bw) - f64(bw).max())
    bwn = e / e.sum()
    w = f64(W_bil)
    t = (mxq(f64(x1).reshape(B * L, D), 1, "e4m3") @ mxq(w[:, :D, :], 1, "e4m3")) + w[:, D, :][:, None, :]
    t = t.reshape(O, B, L, D)
    pair = mxq(t, 3, "e4m3") @ mxq(f64(x2), 2, "e4m3").transpose(0, 2, 1)
    bil = pair.transpose(1, 2, 3, 0) + f64(t_ones)[:, :, None, :]
    lin = f64(lin1)[:, :, None, :] + f64(lin2)[:, None, :, :] + f64(b_lin)
    return bwn[0] * bil + bwn[1] * lin

@@ -1,0 +1,357 @@
+from contextlib import ExitStack
+
+import concourse.mybir as mybir
+from concourse.masks import make_identity
+
+F32 = mybir.dt.float32
+BF16 = mybir.dt.bfloat16
+U32 = mybir.dt.uint32
+U8 = mybir.dt.uint8
+FP8X4 = mybir.dt.float8_e4m3fn_x4
+ACT = mybir.ActivationFunctionType
+ALU = mybir.AluOpType
+
+P = 128
+B, L, D, O = 16, 256, 512, 2
+H = L // P
+
+FLOPS = 2 * B * L * D * O * D + 2 * B * O * L * L * D
+
+LOAD_GROUPS = [(1, 1), (2, 1), (3, 1), (4, 2), (6, 2), (8, 2), (10, 2), (12, 2), (14, 2)]
+LIN2_AFTER = {3: 0, 6: 1, 10: 2, 12: 3}
+
+
+def tile_biaffine_pa_t_kernel(tc, x1, x2, bw, W_bil, t_ones, lin1, lin2, b_lin, out):
+    nc = tc.nc
+    with ExitStack() as ctx:
+        ctx.enter_context(tc.manual_schedule())
+        const = ctx.enter_context(tc.tile_pool(name="const", bufs=1))
+        stage = ctx.enter_context(tc.tile_pool(name="stage", bufs=2))
+        keep3 = ctx.enter_context(tc.tile_pool(name="keep3", bufs=3))
+        keep4 = ctx.enter_context(tc.tile_pool(name="keep4", bufs=4))
+        ps_t = ctx.enter_context(tc.psum_pool(name="ps_t", bufs=2))
+        ps_1 = ctx.enter_context(tc.psum_pool(name="ps_1", bufs=4))
+        ps_2 = ctx.enter_context(tc.psum_pool(name="ps_2", bufs=2))
+
+        sm = const.tile([P, 256], F32, name="sm")
+        nc.vector.memset(sm[:], 0.0)
+        ident = const.tile([P, P], F32, name="ident")
+        make_identity(nc, ident[:])
+
+        w_raw = []
+        for o in range(O):
+            wr = const.tile([P, 4, D], BF16, name="w_raw%d" % o)
+            w_raw.append(wr)
+        x1_raw = {}
+        x2_raw = {}
+
+        def load_w(o):
+            nc.sync.dma_start(
+                out=w_raw[o][:].rearrange("q (u e) j -> q u (e j)", u=2),
+                in_=W_bil[o, 0:D, :].rearrange("(u q e) j -> q u (e j)", u=2, e=2),
+            )
+
+        def load_x(src, store, label, b0, nb):
+            xr = const.tile([P, nb, H * D], BF16, name="%s_raw%d" % (label, b0))
+            nc.sync.dma_start(out=xr[:], in_=src[b0 : b0 + nb].rearrange("b (p h) i -> p b (h i)", h=H))
+            for k in range(nb):
+                store[b0 + k] = (xr, k)
+
+        sm_bf = sm[:].bitcast(BF16)
+        bw_b = const.tile([P, 2], BF16, name="bw_b")
+        bl_b = const.tile([P, 2], BF16, name="bl_b")
+        nc.scalar.dma_start(out=bw_b[:], in_=bw.partition_broadcast(P))
+        nc.scalar.dma_start(out=sm_bf[64:66, :], in_=W_bil[:, D, :])
+        nc.scalar.dma_start(out=sm_bf[0:16, :], in_=t_ones.rearrange("b x o -> b (x o)"))
+        nc.scalar.dma_start(out=sm_bf[32:48, :], in_=lin1.rearrange("b x o -> b (x o)"))
+        nc.scalar.dma_start(out=bl_b[:], in_=b_lin.partition_broadcast(P))
+
+        load_w(0)
+        load_x(x1, x1_raw, "x1", 0, 1)
+        load_w(1)
+        load_x(x2, x2_raw, "x2", 0, 1)
+        lin2_b = const.tile([P, B * L * O], BF16, name="lin2_b")
+        lin2_flat = lin2.rearrange("b y o -> (b y o)")
+        quarter = B * L * O // 4
+        for b0, nb in LOAD_GROUPS:
+            load_x(x1, x1_raw, "x1", b0, nb)
+            load_x(x2, x2_raw, "x2", b0, nb)
+            if b0 in LIN2_AFTER:
+                c0 = LIN2_AFTER[b0] * quarter
+                nc.sync.dma_start(
+                    out=lin2_b[:, c0 : c0 + quarter], in_=lin2_flat[c0 : c0 + quarter].partition_broadcast(P)
+                )
+
+        bwf = const.tile([P, 2], F32, name="bwf")
+        nc.vector.tensor_copy(out=bwf[:], in_=bw_b[:])
+        negm = const.tile([P, 1], F32, name="negm")
+        nc.vector.tensor_tensor(out=negm[:], in0=bwf[:, 0:1], in1=bwf[:, 1:2], op=ALU.max)
+        nc.vector.tensor_scalar_mul(out=negm[:], in0=negm[:], scalar1=-1.0)
+        ebw = const.tile([P, 2], F32, name="ebw")
+        nc.scalar.activation(out=ebw[:], in_=bwf[:], func=ACT.Exp, bias=negm[:], scale=1.0)
+
+        sm_t = ps_t.tile([P, 4, P], F32, name="pt", tag="pt")
+        sm_h = sm[:].rearrange("p (r h) -> p h r", h=H)
+        for h in range(H):
+            nc.tensor.transpose(out=sm_t[:, h, :], in_=sm_h[:, h, :], identity=ident[:])
+        for u in range(2):
+            nc.tensor.transpose(out=sm_t[:, 2 + u, :], in_=sm[:, u * P : (u + 1) * P], identity=ident[:])
+        sm_s = const.tile([P, 4, P], F32, name="sm_s")
+        nc.vector.tensor_copy(out=sm_s[:], in_=sm_t[:])
+        sm_v = sm_s[:].bitcast(BF16).rearrange("p k (row e) -> p k row e", e=2)
+        bias_f = const.tile([P, O, 4], F32, name="bias_f")
+        bias_v = bias_f[:].rearrange("p o (u e) -> p u o e", u=2)
+        for u in range(2):
+            nc.vector.tensor_copy(out=bias_v[:, u], in_=sm_v[:, 2 + u, 64:66, :])
+
+        w_q = const.tile([P, O * D], U32, name="w_q", align_bytes=64)
+        w_s = const.tile([P, O * D], U8, name="w_s", align_bytes=64)
+        w_g = []
+        for o in range(O):
+            wg = const.tile([P, 4 * D], BF16, name="w_g%d" % o, align_bytes=64)
+            w_g.append(wg)
+
+        def regroup_w(o, uj, engine):
+            dst = w_g[o][:].rearrange("q (uj ej m t) -> q uj ej m t", uj=2, ej=2, t=4)
+            src = w_raw[o][:].rearrange("q t (uj m ej) -> q uj ej m t", uj=2, ej=2)
+            if engine == "vector":
+                nc.vector.tensor_copy(out=dst[:, uj], in_=src[:, uj])
+            elif engine == "scalar":
+                nc.scalar.copy(out=dst[:, uj], in_=src[:, uj])
+            else:
+                nc.gpsimd.tensor_scalar(
+                    out=dst[:, uj], in0=src[:, uj], scalar1=1.0, scalar2=0.0, op0=ALU.mult, op1=ALU.add
+                )
+
+        def quant_w(o):
+            nc.vector.quantize_mx(
+                out=w_q[:, o * D : (o + 1) * D].bitcast(FP8X4),
+                scales=w_s[:, o * D : (o + 1) * D],
+                in_=w_g[o][:],
+            )
+
+        pt_x = {}
+        xg = {}
+        xq = {}
+        p1 = {}
+        tg = {}
+        tq = {}
+        p2 = {}
+        tmp = {}
+
+        def transposes(b):
+            for which, store in ((0, x1_raw), (1, x2_raw)):
+                xr, k = store[b]
+                words = xr[:].bitcast(F32)
+                pt = ps_t.tile([P, H, 2, P], F32, name="pt", tag="pt")
+                for h in range(H):
+                    for u in range(2):
+                        c0 = h * 256 + u * P
+                        nc.tensor.transpose(out=pt[:, h, u, :], in_=words[:, k, c0 : c0 + P], identity=ident[:])
+                pt_x[(b, which)] = pt
+
+        def exit_x1(b):
+            x1g = stage.tile([P, 4 * L], BF16, name="x1g", align_bytes=64)
+            nc.scalar.copy(
+                out=x1g[:].bitcast(F32).rearrange("q (h r u) -> q h r u", h=H, u=2),
+                in_=pt_x[(b, 0)][:].rearrange("q h u r -> q h r u"),
+            )
+            xg[(b, 0)] = x1g
+
+        def exit_x2(b):
+            x2g = stage.tile([P, 4 * L], BF16, name="x2g", align_bytes=64)
+            nc.scalar.copy(
+                out=x2g[:].bitcast(F32).rearrange("q (r h u) -> q r h u", h=H, u=2),
+                in_=pt_x[(b, 1)][:].rearrange("q h u r -> q r h u"),
+            )
+            xg[(b, 1)] = x2g
+
+        def quant_x1(b):
+            x1q = keep3.tile([P, L], U32, name="x1q", align_bytes=64)
+            x1s = keep3.tile([P, L], U8, name="x1s", align_bytes=64)
+            nc.vector.quantize_mx(out=x1q[:].bitcast(FP8X4), scales=x1s[:], in_=xg[(b, 0)][:])
+            xq[(b, 0)] = (x1q, x1s)
+
+        def quant_x2(b):
+            x2q = keep4.tile([P, L], U32, name="x2q", align_bytes=64)
+            x2s = keep4.tile([P, L], U8, name="x2s", align_bytes=64)
+            nc.vector.quantize_mx(out=x2q[:].bitcast(FP8X4), scales=x2s[:], in_=xg[(b, 1)][:])
+            xq[(b, 1)] = (x2q, x2s)
+
+        def stage1(b, g):
+            o, h = g // H, g % H
+            x1q, x1s = xq[(b, 0)]
+            acc = ps_1.tile([P, 4, P], F32, name="p1", tag="p1")
+            for c in range(4):
+                w0 = (o * 4 + c) * P
+                nc.tensor.matmul_mx(
+                    out=acc[:, c, :],
+                    lhsT=w_q[:, w0 : w0 + P].bitcast(FP8X4),
+                    lhsT_scale=w_s[:, w0 : w0 + P],
+                    rhs=x1q[:, h * P : (h + 1) * P].bitcast(FP8X4),
+                    rhs_scale=x1s[:, h * P : (h + 1) * P],
+                    start=True,
+                    stop=True,
+                )
+            p1[(b, g)] = acc
+
+        def t_out(b, g):
+            o = g // H
+            if g == 0:
+                tgt = stage.tile([P, 4 * O * L], BF16, name="tg", align_bytes=64)
+                tg[b] = tgt
+            view = tg[b][:].rearrange("q (g r c) -> q g r c", g=O * H, c=4)
+            nc.vector.tensor_tensor(
+                out=view[:, g],
+                in0=p1[(b, g)][:].rearrange("q c r -> q r c"),
+                in1=bias_f[:, o, :].unsqueeze(1).to_broadcast([P, P, 4]),
+                op=ALU.add,
+            )
+
+        def quant_t(b):
+            tqt = stage.tile([P, O * L], U32, name="tq", align_bytes=64)
+            tst = stage.tile([P, O * L], U8, name="ts", align_bytes=64)
+            nc.vector.quantize_mx(out=tqt[:].bitcast(FP8X4), scales=tst[:], in_=tg[b][:])
+            tq[b] = (tqt, tst)
+
+        def stage2(b):
+            tqt, tst = tq[b]
+            x2q, x2s = xq[(b, 1)]
+            for h in range(H):
+                acc = ps_2.tile([P, O, L], F32, name="p2", tag="p2")
+                for o in range(O):
+                    c0 = (o * H + h) * P
+                    nc.tensor.matmul_mx(
+                        out=acc[:, o, :],
+                        lhsT=tqt[:, c0 : c0 + P].bitcast(FP8X4),
+                        lhsT_scale=tst[:, c0 : c0 + P],
+                        rhs=x2q[:].bitcast(FP8X4),
+                        rhs_scale=x2s[:],
+                        start=True,
+                        stop=True,
+                    )
+                p2[(b, h)] = acc
+
+        def pass1(b):
+            tm = keep3.tile([P, H, O, L], F32, name="tmp")
+            for h in range(H):
+                for o in range(O):
+                    nc.scalar.activation(
+                        out=tm[:, h, o, :],
+                        in_=p2[(b, h)][:, o, :],
+                        func=ACT.Identity,
+                        bias=a_x[:, h, b, o : o + 1],
+                        scale=bwn[:, 0:1],
+                    )
+            tmp[b] = tm
+
+        def pass2(b):
+            cb = keep3.tile([P, L, O], F32, name="cb")
+            nc.gpsimd.tensor_scalar(
+                out=cb[:].rearrange("p y o -> p (y o)"),
+                in0=lin2_b[:, b * L * O : (b + 1) * L * O],
+                scalar1=bwn[:, 1:2],
+                scalar2=0.0,
+                op0=ALU.mult,
+                op1=ALU.add,
+            )
+            ot = keep4.tile([P, H, L, O], F32, name="ot")
+            for h in range(H):
+                nc.gpsimd.tensor_tensor(
+                    out=ot[:, h],
+                    in0=tmp[b][:, h].rearrange("p o y -> p y o"),
+                    in1=cb[:],
+                    op=ALU.add,
+                )
+            nc.sync.dma_start(
+                out=out[b].rearrange("(p h) y o -> p (h y o)", h=H),
+                in_=ot[:].rearrange("p h y o -> p (h y o)"),
+            )
+
+        def softmax_tail():
+            nc.vector.tensor_tensor(out=esum[:], in0=ebw[:, 0:1], in1=ebw[:, 1:2], op=ALU.add)
+            nc.vector.reciprocal(out=rsum[:], in_=esum[:])
+            nc.vector.tensor_scalar_mul(out=bwn[:], in0=ebw[:], scalar1=rsum[:])
+            nc.vector.tensor_copy(out=blf[:], in_=bl_b[:])
+            for h in range(H):
+                nc.vector.tensor_tensor(
+                    out=a_x[:, h],
+                    in0=sm_v[:, h, 32:48, :],
+                    in1=blf[:].unsqueeze(1).to_broadcast([P, B, O]),
+                    op=ALU.add,
+                )
+            a_flat = a_x[:].rearrange("p h b o -> p (h b o)")
+            nc.vector.tensor_scalar_mul(out=a_flat, in0=a_flat, scalar1=bwn[:, 1:2])
+            for h in range(H):
+                nc.vector.scalar_tensor_tensor(
+                    out=a_x[:, h],
+                    in0=sm_v[:, h, 0:16, :],
+                    scalar=bwn[:, 0:1],
+                    in1=a_x[:, h],
+                    op0=ALU.mult,
+                    op1=ALU.add,
+                )
+
+        esum = const.tile([P, 1], F32, name="esum")
+        rsum = const.tile([P, 1], F32, name="rsum")
+        bwn = const.tile([P, 2], F32, name="bwn")
+        blf = const.tile([P, 2], F32, name="blf")
+        a_x = const.tile([P, H, B, O], F32, name="a_x")
+
+        regroup_w(0, 0, "vector")
+        regroup_w(0, 1, "vector")
+        transposes(0)
+        exit_x1(0)
+        regroup_w(1, 0, "scalar")
+        regroup_w(1, 1, "gpsimd")
+        exit_x2(0)
+        quant_w(0)
+        quant_x1(0)
+        stage1(0, 0)
+        stage1(0, 1)
+        transposes(1)
+        exit_x1(1)
+        exit_x2(1)
+
+        t_out(0, 0)
+        t_out(0, 1)
+        quant_w(1)
+        quant_x2(0)
+        quant_x1(1)
+        quant_x2(1)
+        softmax_tail()
+        stage1(0, 2)
+        stage1(0, 3)
+        transposes(2)
+        exit_x1(2)
+        exit_x2(2)
+        t_out(0, 2)
+        stage1(1, 0)
+        t_out(0, 3)
+        stage1(1, 1)
+        stage1(1, 2)
+        stage1(1, 3)
+        quant_t(0)
+        quant_x1(2)
+        quant_x2(2)
+        transposes(3)
+
+        for b in range(1, B + 1):
+            stage2(b - 1)
+            if b + 2 < B:
+                exit_x1(b + 2)
+                exit_x2(b + 2)
+            if b < B:
+                for g in range(O * H):
+                    t_out(b, g)
+                    if b + 1 < B:
+                        stage1(b + 1, g)
+            pass1(b - 1)
+            if b + 2 < B:
+                quant_x1(b + 2)
+                quant_x2(b + 2)
+            if b < B:
+                quant_t(b)
+            if b + 3 < B:
+                transposes(b + 3)
+            pass2(b - 1)

@@ -18,7 +18,7 @@ H = L // P
 FLOPS = 2 * B * L * D * O * D + 2 * B * O * L * L * D
 
 LOAD_GROUPS = [(1, 1), (2, 1), (3, 1), (4, 2), (6, 2), (8, 2), (10, 2), (12, 2), (14, 2)]
-LIN2_AFTER = {3: 0, 6: 1, 10: 2, 12: 3}
+REGROUP_ENGINE = "vector"
 
 
 def tile_biaffine_pa_t_kernel(tc, x1, x2, bw, W_bil, t_ones, lin1, lin2, b_lin, out):
@@ -29,14 +29,18 @@ def tile_biaffine_pa_t_kernel(tc, x1, x2, bw, W_bil, t_ones, lin1, lin2, b_lin, 
         stage = ctx.enter_context(tc.tile_pool(name="stage", bufs=2))
         keep3 = ctx.enter_context(tc.tile_pool(name="keep3", bufs=3))
         keep4 = ctx.enter_context(tc.tile_pool(name="keep4", bufs=4))
-        ps_t = ctx.enter_context(tc.psum_pool(name="ps_t", bufs=2))
-        ps_1 = ctx.enter_context(tc.psum_pool(name="ps_1", bufs=4))
+        ps_t = ctx.enter_context(tc.psum_pool(name="ps_t", bufs=4))
+        ps_1 = ctx.enter_context(tc.psum_pool(name="ps_1", bufs=2))
         ps_2 = ctx.enter_context(tc.psum_pool(name="ps_2", bufs=2))
 
         sm = const.tile([P, 256], F32, name="sm")
         nc.vector.memset(sm[:], 0.0)
         ident = const.tile([P, P], F32, name="ident")
         make_identity(nc, ident[:])
+        ident_bf = const.tile([P, P], BF16, name="ident_bf")
+        make_identity(nc, ident_bf[:])
+        l2r = const.tile([P, L * O], BF16, name="l2r")
+        nc.vector.memset(l2r[:], 0.0)
 
         w_raw = []
         for o in range(O):
@@ -64,23 +68,16 @@ def tile_biaffine_pa_t_kernel(tc, x1, x2, bw, W_bil, t_ones, lin1, lin2, b_lin, 
         nc.scalar.dma_start(out=sm_bf[64:66, :], in_=W_bil[:, D, :])
         nc.scalar.dma_start(out=sm_bf[0:16, :], in_=t_ones.rearrange("b x o -> b (x o)"))
         nc.scalar.dma_start(out=sm_bf[32:48, :], in_=lin1.rearrange("b x o -> b (x o)"))
-        nc.scalar.dma_start(out=bl_b[:], in_=b_lin.partition_broadcast(P))
 
         load_w(0)
         load_x(x1, x1_raw, "x1", 0, 1)
         load_w(1)
         load_x(x2, x2_raw, "x2", 0, 1)
-        lin2_b = const.tile([P, B * L * O], BF16, name="lin2_b")
-        lin2_flat = lin2.rearrange("b y o -> (b y o)")
-        quarter = B * L * O // 4
+        nc.scalar.dma_start(out=bl_b[:], in_=b_lin.partition_broadcast(P))
+        nc.scalar.dma_start(out=l2r[0:B, :], in_=lin2.rearrange("b y o -> b (y o)"))
         for b0, nb in LOAD_GROUPS:
             load_x(x1, x1_raw, "x1", b0, nb)
             load_x(x2, x2_raw, "x2", b0, nb)
-            if b0 in LIN2_AFTER:
-                c0 = LIN2_AFTER[b0] * quarter
-                nc.sync.dma_start(
-                    out=lin2_b[:, c0 : c0 + quarter], in_=lin2_flat[c0 : c0 + quarter].partition_broadcast(P)
-                )
 
         bwf = const.tile([P, 2], F32, name="bwf")
         nc.vector.tensor_copy(out=bwf[:], in_=bw_b[:])
@@ -137,7 +134,9 @@ def tile_biaffine_pa_t_kernel(tc, x1, x2, bw, W_bil, t_ones, lin1, lin2, b_lin, 
         tg = {}
         tq = {}
         p2 = {}
-        tmp = {}
+        pp = {}
+        tp = {}
+        st = {}
 
         def transposes(b):
             for which, store in ((0, x1_raw), (1, x2_raw)):
@@ -232,36 +231,74 @@ def tile_biaffine_pa_t_kernel(tc, x1, x2, bw, W_bil, t_ones, lin1, lin2, b_lin, 
                     )
                 p2[(b, h)] = acc
 
-        def pass1(b):
-            tm = keep3.tile([P, H, O, L], F32, name="tmp")
+        def planar_pe(b):
+            x1q, x1s = xq[(b, 0)]
+            for cp in range(2):
+                acc = ps_t.tile([P, 2, L], F32, name="pt", tag="pt")
+                for ci in range(2):
+                    w0 = (4 + 2 * cp + ci) * P
+                    nc.tensor.matmul_mx(
+                        out=acc[:, ci, :],
+                        lhsT=w_q[:, w0 : w0 + P].bitcast(FP8X4),
+                        lhsT_scale=w_s[:, w0 : w0 + P],
+                        rhs=x1q[:].bitcast(FP8X4),
+                        rhs_scale=x1s[:],
+                        start=True,
+                        stop=True,
+                    )
+                pp[(b, cp)] = acc
+
+        def planar_exits(b):
+            tpt = stage.tile([P, 4, L], BF16, name="tp")
+            for c in range(4):
+                nc.scalar.activation(
+                    out=tpt[:, c, :],
+                    in_=pp[(b, c // 2)][:, c % 2, :],
+                    func=ACT.Identity,
+                    bias=bias_f[:, 1, c : c + 1],
+                    scale=1.0,
+                )
+            tp[b] = tpt
+
+        def regroup_t(b):
+            dst = tg[b][:, 4 * L : 8 * L].rearrange("q (xb i t) -> q xb t i", i=4, t=4)
+            src = tp[b][:].rearrange("q t (xb i) -> q xb t i", i=4)
+            if REGROUP_ENGINE == "vector":
+                nc.vector.tensor_copy(out=dst, in_=src)
+            else:
+                nc.gpsimd.tensor_scalar(out=dst, in0=src, scalar1=1.0, scalar2=0.0, op0=ALU.mult, op1=ALU.add)
+
+        def spread_lin2(b):
+            acc = ps_t.tile([P, L, O], F32, name="pt", tag="pt")
+            nc.tensor.matmul(
+                out=acc[:].rearrange("p y o -> p (y o)"),
+                lhsT=ident_bf[:, b : b + 1].to_broadcast([P, P]),
+                rhs=l2r[:],
+                start=True,
+                stop=True,
+            )
+            stt = keep3.tile([P, H, O, L], F32, name="st")
             for h in range(H):
                 for o in range(O):
                     nc.scalar.activation(
-                        out=tm[:, h, o, :],
-                        in_=p2[(b, h)][:, o, :],
+                        out=stt[:, h, o, :],
+                        in_=acc[:, :, o],
                         func=ACT.Identity,
                         bias=a_x[:, h, b, o : o + 1],
-                        scale=bwn[:, 0:1],
+                        scale=bwn[:, 1:2],
                     )
-            tmp[b] = tm
+            st[b] = stt
 
-        def pass2(b):
-            cb = keep3.tile([P, L, O], F32, name="cb")
-            nc.gpsimd.tensor_scalar(
-                out=cb[:].rearrange("p y o -> p (y o)"),
-                in0=lin2_b[:, b * L * O : (b + 1) * L * O],
-                scalar1=bwn[:, 1:2],
-                scalar2=0.0,
-                op0=ALU.mult,
-                op1=ALU.add,
-            )
+        def out_exit(b):
             ot = keep4.tile([P, H, L, O], F32, name="ot")
             for h in range(H):
-                nc.gpsimd.tensor_tensor(
+                nc.vector.scalar_tensor_tensor(
                     out=ot[:, h],
-                    in0=tmp[b][:, h].rearrange("p o y -> p y o"),
-                    in1=cb[:],
-                    op=ALU.add,
+                    in0=p2[(b, h)][:].rearrange("p o y -> p y o"),
+                    scalar=bwn[:, 0:1],
+                    in1=st[b][:, h].rearrange("p o y -> p y o"),
+                    op0=ALU.mult,
+                    op1=ALU.add,
                 )
             nc.sync.dma_start(
                 out=out[b].rearrange("(p h) y o -> p (h y o)", h=H),
@@ -320,20 +357,20 @@ def tile_biaffine_pa_t_kernel(tc, x1, x2, bw, W_bil, t_ones, lin1, lin2, b_lin, 
         quant_x1(1)
         quant_x2(1)
         softmax_tail()
-        stage1(0, 2)
-        stage1(0, 3)
+        planar_pe(0)
+        planar_exits(0)
         transposes(2)
         exit_x1(2)
         exit_x2(2)
-        t_out(0, 2)
+        planar_pe(1)
         stage1(1, 0)
-        t_out(0, 3)
         stage1(1, 1)
-        stage1(1, 2)
-        stage1(1, 3)
-        quant_t(0)
+        planar_exits(1)
+        regroup_t(0)
+        spread_lin2(0)
         quant_x1(2)
         quant_x2(2)
+        quant_t(0)
         transposes(3)
 
         for b in range(1, B + 1):
@@ -341,12 +378,20 @@ def tile_biaffine_pa_t_kernel(tc, x1, x2, bw, W_bil, t_ones, lin1, lin2, b_lin, 
             if b + 2 < B:
                 exit_x1(b + 2)
                 exit_x2(b + 2)
+            if b + 1 < B:
+                planar_pe(b + 1)
             if b < B:
-                for g in range(O * H):
+                for g in range(H):
                     t_out(b, g)
                     if b + 1 < B:
                         stage1(b + 1, g)
-            pass1(b - 1)
+            if b + 1 < B:
+                planar_exits(b + 1)
+            if b < B:
+                regroup_t(b)
+            out_exit(b - 1)
+            if b < B:
+                spread_lin2(b)
             if b + 2 < B:
                 quant_x1(b + 2)
                 quant_x2(b + 2)
@@ -354,4 +399,3 @@ def tile_biaffine_pa_t_kernel(tc, x1, x2, bw, W_bil, t_ones, lin1, lin2, b_lin, 
                 quant_t(b)
             if b + 3 < B:
                 transposes(b + 3)
-            pass2(b - 1)

@@ -18,7 +18,7 @@ H = L // P
 FLOPS = 2 * B * L * D * O * D + 2 * B * O * L * L * D
 
 LOAD_GROUPS = [(1, 1), (2, 1), (3, 1), (4, 2), (6, 2), (8, 2), (10, 2), (12, 2), (14, 2)]
-REGROUP_ENGINE = "vector"
+REGROUP_ENGINE = "gpsimd"
 
 
 def tile_biaffine_pa_t_kernel(tc, x1, x2, bw, W_bil, t_ones, lin1, lin2, b_lin, out):
@@ -194,12 +194,15 @@ def tile_biaffine_pa_t_kernel(tc, x1, x2, bw, W_bil, t_ones, lin1, lin2, b_lin, 
                 )
             p1[(b, g)] = acc
 
-        def t_out(b, g):
-            o = g // H
-            if g == 0:
+        def get_tg(b):
+            if b not in tg:
                 tgt = stage.tile([P, 4 * O * L], BF16, name="tg", align_bytes=64)
                 tg[b] = tgt
-            view = tg[b][:].rearrange("q (g r c) -> q g r c", g=O * H, c=4)
+            return tg[b]
+
+        def t_out(b, g):
+            o = g // H
+            view = get_tg(b)[:].rearrange("q (g r c) -> q g r c", g=O * H, c=4)
             nc.vector.tensor_tensor(
                 out=view[:, g],
                 in0=p1[(b, g)][:].rearrange("q c r -> q r c"),
@@ -261,12 +264,20 @@ def tile_biaffine_pa_t_kernel(tc, x1, x2, bw, W_bil, t_ones, lin1, lin2, b_lin, 
             tp[b] = tpt
 
         def regroup_t(b):
-            dst = tg[b][:, 4 * L : 8 * L].rearrange("q (xb i t) -> q xb t i", i=4, t=4)
+            dst = get_tg(b)[:, 4 * L : 8 * L].rearrange("q (xb i t) -> q xb t i", i=4, t=4)
             src = tp[b][:].rearrange("q t (xb i) -> q xb t i", i=4)
             if REGROUP_ENGINE == "vector":
                 nc.vector.tensor_copy(out=dst, in_=src)
             else:
-                nc.gpsimd.tensor_scalar(out=dst, in0=src, scalar1=1.0, scalar2=0.0, op0=ALU.mult, op1=ALU.add)
+                for k in range(2):
+                    nc.gpsimd.tensor_scalar(
+                        out=dst[:, 32 * k : 32 * k + 32],
+                        in0=src[:, 32 * k : 32 * k + 32],
+                        scalar1=1.0,
+                        scalar2=0.0,
+                        op0=ALU.mult,
+                        op1=ALU.add,
+                    )
 
         def spread_lin2(b):
             acc = ps_t.tile([P, L, O], F32, name="pt", tag="pt")
@@ -359,6 +370,7 @@ def tile_biaffine_pa_t_kernel(tc, x1, x2, bw, W_bil, t_ones, lin1, lin2, b_lin, 
         softmax_tail()
         planar_pe(0)
         planar_exits(0)
+        regroup_t(0)
         transposes(2)
         exit_x1(2)
         exit_x2(2)
@@ -366,7 +378,7 @@ def tile_biaffine_pa_t_kernel(tc, x1, x2, bw, W_bil, t_ones, lin1, lin2, b_lin, 
         stage1(1, 0)
         stage1(1, 1)
         planar_exits(1)
-        regroup_t(0)
+        regroup_t(1)
         spread_lin2(0)
         quant_x1(2)
         quant_x2(2)
@@ -387,8 +399,7 @@ def tile_biaffine_pa_t_kernel(tc, x1, x2, bw, W_bil, t_ones, lin1, lin2, b_lin, 
                         stage1(b + 1, g)
             if b + 1 < B:
                 planar_exits(b + 1)
-            if b < B:
-                regroup_t(b)
+                regroup_t(b + 1)
             out_exit(b - 1)
             if b < B:
                 spread_lin2(b)

@@ -29,6 +29,7 @@ def tile_biaffine_pa_t_kernel(tc, x1, x2, bw, W_bil, t_ones, lin1, lin2, b_lin, 
         stage = ctx.enter_context(tc.tile_pool(name="stage", bufs=2))
         keep3 = ctx.enter_context(tc.tile_pool(name="keep3", bufs=3))
         keep4 = ctx.enter_context(tc.tile_pool(name="keep4", bufs=4))
+        single = ctx.enter_context(tc.tile_pool(name="single", bufs=1))
         ps_t = ctx.enter_context(tc.psum_pool(name="ps_t", bufs=4))
         ps_1 = ctx.enter_context(tc.psum_pool(name="ps_1", bufs=2))
         ps_2 = ctx.enter_context(tc.psum_pool(name="ps_2", bufs=2))
@@ -196,7 +197,7 @@ def tile_biaffine_pa_t_kernel(tc, x1, x2, bw, W_bil, t_ones, lin1, lin2, b_lin, 
 
         def get_tg(b):
             if b not in tg:
-                tgt = stage.tile([P, 4 * O * L], BF16, name="tg", align_bytes=64)
+                tgt = single.tile([P, 4 * O * L], BF16, name="tg", align_bytes=64)
                 tg[b] = tgt
             return tg[b]
 
@@ -378,11 +379,12 @@ def tile_biaffine_pa_t_kernel(tc, x1, x2, bw, W_bil, t_ones, lin1, lin2, b_lin, 
         stage1(1, 0)
         stage1(1, 1)
         planar_exits(1)
-        regroup_t(1)
         spread_lin2(0)
+        spread_lin2(1)
         quant_x1(2)
         quant_x2(2)
         quant_t(0)
+        regroup_t(1)
         transposes(3)
 
         for b in range(1, B + 1):
@@ -399,14 +401,15 @@ def tile_biaffine_pa_t_kernel(tc, x1, x2, bw, W_bil, t_ones, lin1, lin2, b_lin, 
                         stage1(b + 1, g)
             if b + 1 < B:
                 planar_exits(b + 1)
-                regroup_t(b + 1)
             out_exit(b - 1)
-            if b < B:
-                spread_lin2(b)
+            if b + 1 < B:
+                spread_lin2(b + 1)
             if b + 2 < B:
                 quant_x1(b + 2)
                 quant_x2(b + 2)
             if b < B:
                 quant_t(b)
+            if b + 1 < B:
+                regroup_t(b + 1)
             if b + 3 < B:
                 transposes(b + 3)

@@ -270,10 +270,12 @@ def tile_biaffine_pa_t_kernel(tc, x1, x2, bw, W_bil, t_ones, lin1, lin2, b_lin, 
             if REGROUP_ENGINE == "vector":
                 nc.vector.tensor_copy(out=dst, in_=src)
             else:
+                dst = get_tg(b)[:, 4 * L : 8 * L].rearrange("q (x t) -> q x t", t=4)
+                src = tp[b][:].rearrange("q t x -> q x t")
                 for k in range(2):
                     nc.gpsimd.tensor_scalar(
-                        out=dst[:, 32 * k : 32 * k + 32],
-                        in0=src[:, 32 * k : 32 * k + 32],
+                        out=dst[:, P * k : P * k + P],
+                        in0=src[:, P * k : P * k + P],
                         scalar1=1.0,
                         scalar2=0.0,
                         op0=ALU.mult,

@@ -24,12 +24,10 @@ REGROUP_ENGINE = "gpsimd"
 def tile_biaffine_pa_t_kernel(tc, x1, x2, bw, W_bil, t_ones, lin1, lin2, b_lin, out):
     nc = tc.nc
     with ExitStack() as ctx:
-        ctx.enter_context(tc.manual_schedule())
         const = ctx.enter_context(tc.tile_pool(name="const", bufs=1))
         stage = ctx.enter_context(tc.tile_pool(name="stage", bufs=2))
         keep3 = ctx.enter_context(tc.tile_pool(name="keep3", bufs=3))
         keep4 = ctx.enter_context(tc.tile_pool(name="keep4", bufs=4))
-        single = ctx.enter_context(tc.tile_pool(name="single", bufs=1))
         ps_t = ctx.enter_context(tc.psum_pool(name="ps_t", bufs=4))
         ps_1 = ctx.enter_context(tc.psum_pool(name="ps_1", bufs=2))
         ps_2 = ctx.enter_context(tc.psum_pool(name="ps_2", bufs=2))
@@ -197,7 +195,7 @@ def tile_biaffine_pa_t_kernel(tc, x1, x2, bw, W_bil, t_ones, lin1, lin2, b_lin, 
 
         def get_tg(b):
             if b not in tg:
-                tgt = single.tile([P, 4 * O * L], BF16, name="tg", align_bytes=64)
+                tgt = stage.tile([P, 4 * O * L], BF16, name="tg", align_bytes=64)
                 tg[b] = tgt
             return tg[b]
 
@@ -314,10 +312,16 @@ def tile_biaffine_pa_t_kernel(tc, x1, x2, bw, W_bil, t_ones, lin1, lin2, b_lin, 
                     op0=ALU.mult,
                     op1=ALU.add,
                 )
-            nc.sync.dma_start(
-                out=out[b].rearrange("(p h) y o -> p (h y o)", h=H),
-                in_=ot[:].rearrange("p h y o -> p (h y o)"),
-            )
+                if b == B - 1:
+                    nc.sync.dma_start(
+                        out=out[b].rearrange("(p h) y o -> p h (y o)", h=H)[:, h, :],
+                        in_=ot[:, h].rearrange("p y o -> p (y o)"),
+                    )
+            if b < B - 1:
+                nc.sync.dma_start(
+                    out=out[b].rearrange("(p h) y o -> p (h y o)", h=H),
+                    in_=ot[:].rearrange("p h y o -> p (h y o)"),
+                )
 
         def softmax_tail():
             nc.vector.tensor_tensor(out=esum[:], in0=ebw[:, 0:1], in1=ebw[:, 1:2], op=ALU.add)
@@ -381,12 +385,12 @@ def tile_biaffine_pa_t_kernel(tc, x1, x2, bw, W_bil, t_ones, lin1, lin2, b_lin, 
         stage1(1, 0)
         stage1(1, 1)
         planar_exits(1)
+        regroup_t(1)
         spread_lin2(0)
         spread_lin2(1)
         quant_x1(2)
         quant_x2(2)
         quant_t(0)
-        regroup_t(1)
         transposes(3)
 
         for b in range(1, B + 1):
@@ -403,6 +407,7 @@ def tile_biaffine_pa_t_kernel(tc, x1, x2, bw, W_bil, t_ones, lin1, lin2, b_lin, 
                         stage1(b + 1, g)
             if b + 1 < B:
                 planar_exits(b + 1)
+                regroup_t(b + 1)
             out_exit(b - 1)
             if b + 1 < B:
                 spread_lin2(b + 1)
@@ -411,7 +416,5 @@ def tile_biaffine_pa_t_kernel(tc, x1, x2, bw, W_bil, t_ones, lin1, lin2, b_lin, 
                 quant_x2(b + 2)
             if b < B:
                 quant_t(b)
-            if b + 1 < B:
-                regroup_t(b + 1)
             if b + 3 < B:
                 transposes(b + 3)

@@ -19,6 +19,7 @@ FLOPS = 2 * B * L * D * O * D + 2 * B * O * L * L * D
 
 LOAD_GROUPS = [(1, 1), (2, 1), (3, 1), (4, 2), (6, 2), (8, 2), (10, 2), (12, 2), (14, 2)]
 REGROUP_ENGINE = "gpsimd"
+BOTH_PLANAR = (3, 7, 11, 14)
 
 
 def tile_biaffine_pa_t_kernel(tc, x1, x2, bw, W_bil, t_ones, lin1, lin2, b_lin, out):
@@ -107,28 +108,31 @@ def tile_biaffine_pa_t_kernel(tc, x1, x2, bw, W_bil, t_ones, lin1, lin2, b_lin, 
             wg = const.tile([P, 4 * D], BF16, name="w_g%d" % o, align_bytes=64)
             w_g.append(wg)
 
-        def regroup_w(o, uj, engine):
-            dst = w_g[o][:].rearrange("q (uj ej m t) -> q uj ej m t", uj=2, ej=2, t=4)
-            src = w_raw[o][:].rearrange("q t (uj m ej) -> q uj ej m t", uj=2, ej=2)
+        def regroup_w(o, uj, ej, engine):
+            dst = w_g[o][:].rearrange("q (uj ej m t) -> q uj ej m t", uj=2, ej=2, t=4)[:, uj]
+            src = w_raw[o][:].rearrange("q t (uj m ej) -> q uj ej m t", uj=2, ej=2)[:, uj]
+            if ej is not None:
+                dst = dst[:, ej]
+                src = src[:, ej]
             if engine == "vector":
-                nc.vector.tensor_copy(out=dst[:, uj], in_=src[:, uj])
+                nc.vector.tensor_copy(out=dst, in_=src)
             elif engine == "scalar":
-                nc.scalar.copy(out=dst[:, uj], in_=src[:, uj])
+                nc.scalar.copy(out=dst, in_=src)
             else:
-                nc.gpsimd.tensor_scalar(
-                    out=dst[:, uj], in0=src[:, uj], scalar1=1.0, scalar2=0.0, op0=ALU.mult, op1=ALU.add
-                )
+                nc.gpsimd.tensor_scalar(out=dst, in0=src, scalar1=1.0, scalar2=0.0, op0=ALU.mult, op1=ALU.add)
 
-        def quant_w(o):
-            nc.vector.quantize_mx(
-                out=w_q[:, o * D : (o + 1) * D].bitcast(FP8X4),
-                scales=w_s[:, o * D : (o + 1) * D],
-                in_=w_g[o][:],
-            )
+        def quant_w(o, uj):
+            c0, c1 = o * D, (o + 1) * D
+            g0, g1 = 0, 4 * D
+            if uj is not None:
+                c0, c1 = o * D + uj * (D // 2), o * D + (uj + 1) * (D // 2)
+                g0, g1 = uj * 2 * D, (uj + 1) * 2 * D
+            nc.vector.quantize_mx(out=w_q[:, c0:c1].bitcast(FP8X4), scales=w_s[:, c0:c1], in_=w_g[o][:, g0:g1])
 
         pt_x = {}
         xg = {}
         xq = {}
+        xq_tiles = {}
         p1 = {}
         tg = {}
         tq = {}
@@ -149,32 +153,36 @@ def tile_biaffine_pa_t_kernel(tc, x1, x2, bw, W_bil, t_ones, lin1, lin2, b_lin, 
                 pt_x[(b, which)] = pt
 
         def exit_x1(b):
-            x1g = stage.tile([P, 4 * L], BF16, name="x1g", align_bytes=64)
+            xgt = stage.tile([P, 2, 4 * L], BF16, name="xg", align_bytes=64)
+            xg[b] = xgt
             nc.scalar.copy(
-                out=x1g[:].bitcast(F32).rearrange("q (h r u) -> q h r u", h=H, u=2),
+                out=xgt[:, 0, :].bitcast(F32).rearrange("q (h r u) -> q h r u", h=H, u=2),
                 in_=pt_x[(b, 0)][:].rearrange("q h u r -> q h r u"),
             )
-            xg[(b, 0)] = x1g
 
         def exit_x2(b):
-            x2g = stage.tile([P, 4 * L], BF16, name="x2g", align_bytes=64)
             nc.scalar.copy(
-                out=x2g[:].bitcast(F32).rearrange("q (r h u) -> q r h u", h=H, u=2),
+                out=xg[b][:, 1, :].bitcast(F32).rearrange("q (r h u) -> q r h u", h=H, u=2),
                 in_=pt_x[(b, 1)][:].rearrange("q h u r -> q r h u"),
             )
-            xg[(b, 1)] = x2g
 
-        def quant_x1(b):
-            x1q = keep3.tile([P, L], U32, name="x1q", align_bytes=64)
-            x1s = keep3.tile([P, L], U8, name="x1s", align_bytes=64)
-            nc.vector.quantize_mx(out=x1q[:].bitcast(FP8X4), scales=x1s[:], in_=xg[(b, 0)][:])
-            xq[(b, 0)] = (x1q, x1s)
-
-        def quant_x2(b):
-            x2q = keep4.tile([P, L], U32, name="x2q", align_bytes=64)
-            x2s = keep4.tile([P, L], U8, name="x2s", align_bytes=64)
-            nc.vector.quantize_mx(out=x2q[:].bitcast(FP8X4), scales=x2s[:], in_=xg[(b, 1)][:])
-            xq[(b, 1)] = (x2q, x2s)
+        def quant_x(b, parts):
+            if b not in xq_tiles:
+                xqt = keep4.tile([P, 2, L], U32, name="xq", align_bytes=64)
+                xst = keep4.tile([P, 2, L], U8, name="xs", align_bytes=64)
+                xq_tiles[b] = (xqt, xst)
+                for w in range(2):
+                    xq[(b, w)] = (xqt[:, w, :], xst[:, w, :])
+            xqt, xst = xq_tiles[b]
+            for w in parts:
+                if w is None:
+                    nc.vector.quantize_mx(
+                        out=xqt[:].rearrange("q w c -> q (w c)").bitcast(FP8X4),
+                        scales=xst[:].rearrange("q w c -> q (w c)"),
+                        in_=xg[b][:].rearrange("q w c -> q (w c)"),
+                    )
+                else:
+                    nc.vector.quantize_mx(out=xqt[:, w, :].bitcast(FP8X4), scales=xst[:, w, :], in_=xg[b][:, w, :])
 
         def stage1(b, g):
             o, h = g // H, g % H
@@ -226,50 +234,51 @@ def tile_biaffine_pa_t_kernel(tc, x1, x2, bw, W_bil, t_ones, lin1, lin2, b_lin, 
                         out=acc[:, o, :],
                         lhsT=tqt[:, c0 : c0 + P].bitcast(FP8X4),
                         lhsT_scale=tst[:, c0 : c0 + P],
-                        rhs=x2q[:].bitcast(FP8X4),
-                        rhs_scale=x2s[:],
+                        rhs=x2q.bitcast(FP8X4),
+                        rhs_scale=x2s,
                         start=True,
                         stop=True,
                     )
                 p2[(b, h)] = acc
 
-        def planar_pe(b):
+        def planar_pe(b, o):
             x1q, x1s = xq[(b, 0)]
             for cp in range(2):
                 acc = ps_t.tile([P, 2, L], F32, name="pt", tag="pt")
                 for ci in range(2):
-                    w0 = (4 + 2 * cp + ci) * P
+                    w0 = (4 * o + 2 * cp + ci) * P
                     nc.tensor.matmul_mx(
                         out=acc[:, ci, :],
                         lhsT=w_q[:, w0 : w0 + P].bitcast(FP8X4),
                         lhsT_scale=w_s[:, w0 : w0 + P],
-                        rhs=x1q[:].bitcast(FP8X4),
-                        rhs_scale=x1s[:],
+                        rhs=x1q.bitcast(FP8X4),
+                        rhs_scale=x1s,
                         start=True,
                         stop=True,
                     )
-                pp[(b, cp)] = acc
+                pp[(b, o, cp)] = acc
 
-        def planar_exits(b):
-            tpt = stage.tile([P, 4, L], BF16, name="tp")
+        def planar_exits(b, o):
+            tpt = keep3.tile([P, 4, L], BF16, name="tp")
             for c in range(4):
                 nc.scalar.activation(
                     out=tpt[:, c, :],
-                    in_=pp[(b, c // 2)][:, c % 2, :],
+                    in_=pp[(b, o, c // 2)][:, c % 2, :],
                     func=ACT.Identity,
-                    bias=bias_f[:, 1, c : c + 1],
+                    bias=bias_f[:, o, c : c + 1],
                     scale=1.0,
                 )
-            tp[b] = tpt
+            tp[(b, o)] = tpt
 
-        def regroup_t(b):
-            dst = get_tg(b)[:, 4 * L : 8 * L].rearrange("q (xb i t) -> q xb t i", i=4, t=4)
-            src = tp[b][:].rearrange("q t (xb i) -> q xb t i", i=4)
+        def regroup_t(b, o):
+            half = get_tg(b)[:, 4 * L * o : 4 * L * (o + 1)]
+            dst = half.rearrange("q (xb i t) -> q xb t i", i=4, t=4)
+            src = tp[(b, o)][:].rearrange("q t (xb i) -> q xb t i", i=4)
             if REGROUP_ENGINE == "vector":
                 nc.vector.tensor_copy(out=dst, in_=src)
             else:
-                dst = get_tg(b)[:, 4 * L : 8 * L].rearrange("q (x t) -> q x t", t=4)
-                src = tp[b][:].rearrange("q t x -> q x t")
+                dst = half.rearrange("q (x t) -> q x t", t=4)
+                src = tp[(b, o)][:].rearrange("q t x -> q x t")
                 for k in range(2):
                     nc.gpsimd.tensor_scalar(
                         out=dst[:, P * k : P * k + P],
@@ -353,15 +362,15 @@ def tile_biaffine_pa_t_kernel(tc, x1, x2, bw, W_bil, t_ones, lin1, lin2, b_lin, 
         blf = const.tile([P, 2], F32, name="blf")
         a_x = const.tile([P, H, B, O], F32, name="a_x")
 
-        regroup_w(0, 0, "vector")
-        regroup_w(0, 1, "vector")
+        regroup_w(0, 0, None, "vector")
+        regroup_w(0, 1, None, "vector")
         transposes(0)
         exit_x1(0)
-        regroup_w(1, 0, "scalar")
-        regroup_w(1, 1, "gpsimd")
+        regroup_w(1, 0, None, "scalar")
+        regroup_w(1, 1, None, "gpsimd")
         exit_x2(0)
-        quant_w(0)
-        quant_x1(0)
+        quant_w(0, None)
+        quant_x(0, (0,))
         stage1(0, 0)
         stage1(0, 1)
         transposes(1)
@@ -370,26 +379,24 @@ def tile_biaffine_pa_t_kernel(tc, x1, x2, bw, W_bil, t_ones, lin1, lin2, b_lin, 
 
         t_out(0, 0)
         t_out(0, 1)
-        quant_w(1)
-        quant_x2(0)
-        quant_x1(1)
-        quant_x2(1)
+        quant_w(1, None)
+        quant_x(0, (1,))
+        quant_x(1, (None,))
         softmax_tail()
-        planar_pe(0)
-        planar_exits(0)
-        regroup_t(0)
+        planar_pe(0, 1)
+        planar_exits(0, 1)
+        regroup_t(0, 1)
         transposes(2)
         exit_x1(2)
         exit_x2(2)
-        planar_pe(1)
+        planar_pe(1, 1)
         stage1(1, 0)
         stage1(1, 1)
-        planar_exits(1)
-        regroup_t(1)
+        planar_exits(1, 1)
+        regroup_t(1, 1)
         spread_lin2(0)
         spread_lin2(1)
-        quant_x1(2)
-        quant_x2(2)
+        quant_x(2, (None,))
         quant_t(0)
         transposes(3)
 
@@ -399,21 +406,23 @@ def tile_biaffine_pa_t_kernel(tc, x1, x2, bw, W_bil, t_ones, lin1, lin2, b_lin, 
                 exit_x1(b + 2)
                 exit_x2(b + 2)
             if b + 1 < B:
-                planar_pe(b + 1)
-            if b < B:
-                for g in range(H):
+                planar_pe(b + 1, 1)
+                planar_exits(b + 1, 1)
+                regroup_t(b + 1, 1)
+                if b + 1 in BOTH_PLANAR:
+                    planar_pe(b + 1, 0)
+                    planar_exits(b + 1, 0)
+                    regroup_t(b + 1, 0)
+            for g in range(H):
+                if b < B and b not in BOTH_PLANAR:
                     t_out(b, g)
-                    if b + 1 < B:
-                        stage1(b + 1, g)
-            if b + 1 < B:
-                planar_exits(b + 1)
-                regroup_t(b + 1)
+                if b + 1 < B and b + 1 not in BOTH_PLANAR:
+                    stage1(b + 1, g)
             out_exit(b - 1)
             if b + 1 < B:
                 spread_lin2(b + 1)
             if b + 2 < B:
-                quant_x1(b + 2)
-                quant_x2(b + 2)
+                quant_x(b + 2, (None,))
             if b < B:
                 quant_t(b)
             if b + 3 < B:

@@ -19,7 +19,7 @@ FLOPS = 2 * B * L * D * O * D + 2 * B * O * L * L * D
 
 LOAD_GROUPS = [(1, 1), (2, 1), (3, 1), (4, 2), (6, 2), (8, 2), (10, 2), (12, 2), (14, 2)]
 REGROUP_ENGINE = "gpsimd"
-BOTH_PLANAR = (3, 7, 11, 14)
+BOTH_PLANAR = ()
 
 
 def tile_biaffine_pa_t_kernel(tc, x1, x2, bw, W_bil, t_ones, lin1, lin2, b_lin, out):

from contextlib import ExitStack

import concourse.mybir as mybir
from concourse.masks import make_identity

F32 = mybir.dt.float32
BF16 = mybir.dt.bfloat16
U32 = mybir.dt.uint32
U8 = mybir.dt.uint8
FP8X4 = mybir.dt.float8_e4m3fn_x4
ACT = mybir.ActivationFunctionType
ALU = mybir.AluOpType

P = 128
B, L, D, O = 16, 256, 512, 2
H = L // P

FLOPS = 2 * B * L * D * O * D + 2 * B * O * L * L * D

LOAD_GROUPS = [(1, 1), (2, 1), (3, 1), (4, 2), (6, 2), (8, 2), (10, 2), (12, 2), (14, 2)]
REGROUP_ENGINE = "gpsimd"
BOTH_PLANAR = ()


def tile_biaffine_pa_t_kernel(tc, x1, x2, bw, W_bil, t_ones, lin1, lin2, b_lin, out):
    nc = tc.nc
    with ExitStack() as ctx:
        const = ctx.enter_context(tc.tile_pool(name="const", bufs=1))
        stage = ctx.enter_context(tc.tile_pool(name="stage", bufs=2))
        keep3 = ctx.enter_context(tc.tile_pool(name="keep3", bufs=3))
        keep4 = ctx.enter_context(tc.tile_pool(name="keep4", bufs=4))
        ps_t = ctx.enter_context(tc.psum_pool(name="ps_t", bufs=4))
        ps_1 = ctx.enter_context(tc.psum_pool(name="ps_1", bufs=2))
        ps_2 = ctx.enter_context(tc.psum_pool(name="ps_2", bufs=2))

        sm = const.tile([P, 256], F32, name="sm")
        nc.vector.memset(sm[:], 0.0)
        ident = const.tile([P, P], F32, name="ident")
        make_identity(nc, ident[:])
        ident_bf = const.tile([P, P], BF16, name="ident_bf")
        make_identity(nc, ident_bf[:])
        l2r = const.tile([P, L * O], BF16, name="l2r")
        nc.vector.memset(l2r[:], 0.0)

        w_raw = []
        for o in range(O):
            wr = const.tile([P, 4, D], BF16, name="w_raw%d" % o)
            w_raw.append(wr)
        x1_raw = {}
        x2_raw = {}

        def load_w(o):
            nc.sync.dma_start(
                out=w_raw[o][:].rearrange("q (u e) j -> q u (e j)", u=2),
                in_=W_bil[o, 0:D, :].rearrange("(u q e) j -> q u (e j)", u=2, e=2),
            )

        def load_x(src, store, label, b0, nb):
            xr = const.tile([P, nb, H * D], BF16, name="%s_raw%d" % (label, b0))
            nc.sync.dma_start(out=xr[:], in_=src[b0 : b0 + nb].rearrange("b (p h) i -> p b (h i)", h=H))
            for k in range(nb):
                store[b0 + k] = (xr, k)

        sm_bf = sm[:].bitcast(BF16)
        bw_b = const.tile([P, 2], BF16, name="bw_b")
        bl_b = const.tile([P, 2], BF16, name="bl_b")
        nc.scalar.dma_start(out=bw_b[:], in_=bw.partition_broadcast(P))
        nc.scalar.dma_start(out=sm_bf[64:66, :], in_=W_bil[:, D, :])
        nc.scalar.dma_start(out=sm_bf[0:16, :], in_=t_ones.rearrange("b x o -> b (x o)"))
        nc.scalar.dma_start(out=sm_bf[32:48, :], in_=lin1.rearrange("b x o -> b (x o)"))

        load_w(0)
        load_x(x1, x1_raw, "x1", 0, 1)
        load_w(1)
        load_x(x2, x2_raw, "x2", 0, 1)
        nc.scalar.dma_start(out=bl_b[:], in_=b_lin.partition_broadcast(P))
        nc.scalar.dma_start(out=l2r[0:B, :], in_=lin2.rearrange("b y o -> b (y o)"))
        for b0, nb in LOAD_GROUPS:
            load_x(x1, x1_raw, "x1", b0, nb)
            load_x(x2, x2_raw, "x2", b0, nb)

        bwf = const.tile([P, 2], F32, name="bwf")
        nc.vector.tensor_copy(out=bwf[:], in_=bw_b[:])
        negm = const.tile([P, 1], F32, name="negm")
        nc.vector.tensor_tensor(out=negm[:], in0=bwf[:, 0:1], in1=bwf[:, 1:2], op=ALU.max)
        nc.vector.tensor_scalar_mul(out=negm[:], in0=negm[:], scalar1=-1.0)
        ebw = const.tile([P, 2], F32, name="ebw")
        nc.scalar.activation(out=ebw[:], in_=bwf[:], func=ACT.Exp, bias=negm[:], scale=1.0)

        sm_t = ps_t.tile([P, 4, P], F32, name="pt", tag="pt")
        sm_h = sm[:].rearrange("p (r h) -> p h r", h=H)
        for h in range(H):
            nc.tensor.transpose(out=sm_t[:, h, :], in_=sm_h[:, h, :], identity=ident[:])
        for u in range(2):
            nc.tensor.transpose(out=sm_t[:, 2 + u, :], in_=sm[:, u * P : (u + 1) * P], identity=ident[:])
        sm_s = const.tile([P, 4, P], F32, name="sm_s")
        nc.vector.tensor_copy(out=sm_s[:], in_=sm_t[:])
        sm_v = sm_s[:].bitcast(BF16).rearrange("p k (row e) -> p k row e", e=2)
        bias_f = const.tile([P, O, 4], F32, name="bias_f")
        bias_v = bias_f[:].rearrange("p o (u e) -> p u o e", u=2)
        for u in range(2):
            nc.vector.tensor_copy(out=bias_v[:, u], in_=sm_v[:, 2 + u, 64:66, :])

        w_q = const.tile([P, O * D], U32, name="w_q", align_bytes=64)
        w_s = const.tile([P, O * D], U8, name="w_s", align_bytes=64)
        w_g = []
        for o in range(O):
            wg = const.tile([P, 4 * D], BF16, name="w_g%d" % o, align_bytes=64)
            w_g.append(wg)

        def regroup_w(o, uj, ej, engine):
            dst = w_g[o][:].rearrange("q (uj ej m t) -> q uj ej m t", uj=2, ej=2, t=4)[:, uj]
            src = w_raw[o][:].rearrange("q t (uj m ej) -> q uj ej m t", uj=2, ej=2)[:, uj]
            if ej is not None:
                dst = dst[:, ej]
                src = src[:, ej]
            if engine == "vector":
                nc.vector.tensor_copy(out=dst, in_=src)
            elif engine == "scalar":
                nc.scalar.copy(out=dst, in_=src)
            else:
                nc.gpsimd.tensor_scalar(out=dst, in0=src, scalar1=1.0, scalar2=0.0, op0=ALU.mult, op1=ALU.add)

        def quant_w(o, uj):
            c0, c1 = o * D, (o + 1) * D
            g0, g1 = 0, 4 * D
            if uj is not None:
                c0, c1 = o * D + uj * (D // 2), o * D + (uj + 1) * (D // 2)
                g0, g1 = uj * 2 * D, (uj + 1) * 2 * D
            nc.vector.quantize_mx(out=w_q[:, c0:c1].bitcast(FP8X4), scales=w_s[:, c0:c1], in_=w_g[o][:, g0:g1])

        pt_x = {}
        xg = {}
        xq = {}
        xq_tiles = {}
        p1 = {}
        tg = {}
        tq = {}
        p2 = {}
        pp = {}
        tp = {}
        st = {}

        def transposes(b):
            for which, store in ((0, x1_raw), (1, x2_raw)):
                xr, k = store[b]
                words = xr[:].bitcast(F32)
                pt = ps_t.tile([P, H, 2, P], F32, name="pt", tag="pt")
                for h in range(H):
                    for u in range(2):
                        c0 = h * 256 + u * P
                        nc.tensor.transpose(out=pt[:, h, u, :], in_=words[:, k, c0 : c0 + P], identity=ident[:])
                pt_x[(b, which)] = pt

        def exit_x1(b):
            xgt = stage.tile([P, 2, 4 * L], BF16, name="xg", align_bytes=64)
            xg[b] = xgt
            nc.scalar.copy(
                out=xgt[:, 0, :].bitcast(F32).rearrange("q (h r u) -> q h r u", h=H, u=2),
                in_=pt_x[(b, 0)][:].rearrange("q h u r -> q h r u"),
            )

        def exit_x2(b):
            nc.scalar.copy(
                out=xg[b][:, 1, :].bitcast(F32).rearrange("q (r h u) -> q r h u", h=H, u=2),
                in_=pt_x[(b, 1)][:].rearrange("q h u r -> q r h u"),
            )

        def quant_x(b, parts):
            if b not in xq_tiles:
                xqt = keep4.tile([P, 2, L], U32, name="xq", align_bytes=64)
                xst = keep4.tile([P, 2, L], U8, name="xs", align_bytes=64)
                xq_tiles[b] = (xqt, xst)
                for w in range(2):
                    xq[(b, w)] = (xqt[:, w, :], xst[:, w, :])
            xqt, xst = xq_tiles[b]
            for w in parts:
                if w is None:
                    nc.vector.quantize_mx(
                        out=xqt[:].rearrange("q w c -> q (w c)").bitcast(FP8X4),
                        scales=xst[:].rearrange("q w c -> q (w c)"),
                        in_=xg[b][:].rearrange("q w c -> q (w c)"),
                    )
                else:
                    nc.vector.quantize_mx(out=xqt[:, w, :].bitcast(FP8X4), scales=xst[:, w, :], in_=xg[b][:, w, :])

        def stage1(b, g):
            o, h = g // H, g % H
            x1q, x1s = xq[(b, 0)]
            acc = ps_1.tile([P, 4, P], F32, name="p1", tag="p1")
            for c in range(4):
                w0 = (o * 4 + c) * P
                nc.tensor.matmul_mx(
                    out=acc[:, c, :],
                    lhsT=w_q[:, w0 : w0 + P].bitcast(FP8X4),
                    lhsT_scale=w_s[:, w0 : w0 + P],
                    rhs=x1q[:, h * P : (h + 1) * P].bitcast(FP8X4),
                    rhs_scale=x1s[:, h * P : (h + 1) * P],
                    start=True,
                    stop=True,
                )
            p1[(b, g)] = acc

        def get_tg(b):
            if b not in tg:
                tgt = stage.tile([P, 4 * O * L], BF16, name="tg", align_bytes=64)
                tg[b] = tgt
            return tg[b]

        def t_out(b, g):
            o = g // H
            view = get_tg(b)[:].rearrange("q (g r c) -> q g r c", g=O * H, c=4)
            nc.vector.tensor_tensor(
                out=view[:, g],
                in0=p1[(b, g)][:].rearrange("q c r -> q r c"),
                in1=bias_f[:, o, :].unsqueeze(1).to_broadcast([P, P, 4]),
                op=ALU.add,
            )

        def quant_t(b):
            tqt = stage.tile([P, O * L], U32, name="tq", align_bytes=64)
            tst = stage.tile([P, O * L], U8, name="ts", align_bytes=64)
            nc.vector.quantize_mx(out=tqt[:].bitcast(FP8X4), scales=tst[:], in_=tg[b][:])
            tq[b] = (tqt, tst)

        def stage2(b):
            tqt, tst = tq[b]
            x2q, x2s = xq[(b, 1)]
            for h in range(H):
                acc = ps_2.tile([P, O, L], F32, name="p2", tag="p2")
                for o in range(O):
                    c0 = (o * H + h) * P
                    nc.tensor.matmul_mx(
                        out=acc[:, o, :],
                        lhsT=tqt[:, c0 : c0 + P].bitcast(FP8X4),
                        lhsT_scale=tst[:, c0 : c0 + P],
                        rhs=x2q.bitcast(FP8X4),
                        rhs_scale=x2s,
                        start=True,
                        stop=True,
                    )
                p2[(b, h)] = acc

        def planar_pe(b, o):
            x1q, x1s = xq[(b, 0)]
            for cp in range(2):
                acc = ps_t.tile([P, 2, L], F32, name="pt", tag="pt")
                for ci in range(2):
                    w0 = (4 * o + 2 * cp + ci) * P
                    nc.tensor.matmul_mx(
                        out=acc[:, ci, :],
                        lhsT=w_q[:, w0 : w0 + P].bitcast(FP8X4),
                        lhsT_scale=w_s[:, w0 : w0 + P],
                        rhs=x1q.bitcast(FP8X4),
                        rhs_scale=x1s,
                        start=True,
                        stop=True,
                    )
                pp[(b, o, cp)] = acc

        def planar_exits(b, o):
            tpt = keep3.tile([P, 4, L], BF16, name="tp")
            for c in range(4):
                nc.scalar.activation(
                    out=tpt[:, c, :],
                    in_=pp[(b, o, c // 2)][:, c % 2, :],
                    func=ACT.Identity,
                    bias=bias_f[:, o, c : c + 1],
                    scale=1.0,
                )
            tp[(b, o)] = tpt

        def regroup_t(b, o):
            half = get_tg(b)[:, 4 * L * o : 4 * L * (o + 1)]
            dst = half.rearrange("q (xb i t) -> q xb t i", i=4, t=4)
            src = tp[(b, o)][:].rearrange("q t (xb i) -> q xb t i", i=4)
            if REGROUP_ENGINE == "vector":
                nc.vector.tensor_copy(out=dst, in_=src)
            else:
                dst = half.rearrange("q (x t) -> q x t", t=4)
                src = tp[(b, o)][:].rearrange("q t x -> q x t")
                for k in range(2):
                    nc.gpsimd.tensor_scalar(
                        out=dst[:, P * k : P * k + P],
                        in0=src[:, P * k : P * k + P],
                        scalar1=1.0,
                        scalar2=0.0,
                        op0=ALU.mult,
                        op1=ALU.add,
                    )

        def spread_lin2(b):
            acc = ps_t.tile([P, L, O], F32, name="pt", tag="pt")
            nc.tensor.matmul(
                out=acc[:].rearrange("p y o -> p (y o)"),
                lhsT=ident_bf[:, b : b + 1].to_broadcast([P, P]),
                rhs=l2r[:],
                start=True,
                stop=True,
            )
            stt = keep3.tile([P, H, O, L], F32, name="st")
            for h in range(H):
                for o in range(O):
                    nc.scalar.activation(
                        out=stt[:, h, o, :],
                        in_=acc[:, :, o],
                        func=ACT.Identity,
                        bias=a_x[:, h, b, o : o + 1],
                        scale=bwn[:, 1:2],
                    )
            st[b] = stt

        def out_exit(b):
            ot = keep4.tile([P, H, L, O], F32, name="ot")
            for h in range(H):
                nc.vector.scalar_tensor_tensor(
                    out=ot[:, h],
                    in0=p2[(b, h)][:].rearrange("p o y -> p y o"),
                    scalar=bwn[:, 0:1],
                    in1=st[b][:, h].rearrange("p o y -> p y o"),
                    op0=ALU.mult,
                    op1=ALU.add,
                )
                if b == B - 1:
                    nc.sync.dma_start(
                        out=out[b].rearrange("(p h) y o -> p h (y o)", h=H)[:, h, :],
                        in_=ot[:, h].rearrange("p y o -> p (y o)"),
                    )
            if b < B - 1:
                nc.sync.dma_start(
                    out=out[b].rearrange("(p h) y o -> p (h y o)", h=H),
                    in_=ot[:].rearrange("p h y o -> p (h y o)"),
                )

        def softmax_tail():
            nc.vector.tensor_tensor(out=esum[:], in0=ebw[:, 0:1], in1=ebw[:, 1:2], op=ALU.add)
            nc.vector.reciprocal(out=rsum[:], in_=esum[:])
            nc.vector.tensor_scalar_mul(out=bwn[:], in0=ebw[:], scalar1=rsum[:])
            nc.vector.tensor_copy(out=blf[:], in_=bl_b[:])
            for h in range(H):
                nc.vector.tensor_tensor(
                    out=a_x[:, h],
                    in0=sm_v[:, h, 32:48, :],
                    in1=blf[:].unsqueeze(1).to_broadcast([P, B, O]),
                    op=ALU.add,
                )
            a_flat = a_x[:].rearrange("p h b o -> p (h b o)")
            nc.vector.tensor_scalar_mul(out=a_flat, in0=a_flat, scalar1=bwn[:, 1:2])
            for h in range(H):
                nc.vector.scalar_tensor_tensor(
                    out=a_x[:, h],
                    in0=sm_v[:, h, 0:16, :],
                    scalar=bwn[:, 0:1],
                    in1=a_x[:, h],
                    op0=ALU.mult,
                    op1=ALU.add,
                )

        esum = const.tile([P, 1], F32, name="esum")
        rsum = const.tile([P, 1], F32, name="rsum")
        bwn = const.tile([P, 2], F32, name="bwn")
        blf = const.tile([P, 2], F32, name="blf")
        a_x = const.tile([P, H, B, O], F32, name="a_x")

        regroup_w(0, 0, None, "vector")
        regroup_w(0, 1, None, "vector")
        transposes(0)
        exit_x1(0)
        regroup_w(1, 0, None, "scalar")
        regroup_w(1, 1, None, "gpsimd")
        exit_x2(0)
        quant_w(0, None)
        quant_x(0, (0,))
        stage1(0, 0)
        stage1(0, 1)
        transposes(1)
        exit_x1(1)
        exit_x2(1)

        t_out(0, 0)
        t_out(0, 1)
        quant_w(1, None)
        quant_x(0, (1,))
        quant_x(1, (None,))
        softmax_tail()
        planar_pe(0, 1)
        planar_exits(0, 1)
        regroup_t(0, 1)
        transposes(2)
        exit_x1(2)
        exit_x2(2)
        planar_pe(1, 1)
        stage1(1, 0)
        stage1(1, 1)
        planar_exits(1, 1)
        regroup_t(1, 1)
        spread_lin2(0)
        spread_lin2(1)
        quant_x(2, (None,))
        quant_t(0)
        transposes(3)

        for b in range(1, B + 1):
            stage2(b - 1)
            if b + 2 < B:
                exit_x1(b + 2)
                exit_x2(b + 2)
            if b + 1 < B:
                planar_pe(b + 1, 1)
                planar_exits(b + 1, 1)
                regroup_t(b + 1, 1)
                if b + 1 in BOTH_PLANAR:
                    planar_pe(b + 1, 0)
                    planar_exits(b + 1, 0)
                    regroup_t(b + 1, 0)
            for g in range(H):
                if b < B and b not in BOTH_PLANAR:
                    t_out(b, g)
                if b + 1 < B and b + 1 not in BOTH_PLANAR:
                    stage1(b + 1, g)
            out_exit(b - 1)
            if b + 1 < B:
                spread_lin2(b + 1)
            if b + 2 < B:
                quant_x(b + 2, (None,))
            if b < B:
                quant_t(b)
            if b + 3 < B:
                transposes(b + 3)
